import numpy as np
import ml_dtypes

BF16 = ml_dtypes.bfloat16


def bf(x):
    return np.asarray(x, np.float32).astype(BF16)


def f32(x):
    return np.asarray(x, np.float32)


def f64(x):
    return np.asarray(x).astype(np.float64)


def striped(idx):
    return np.tile(idx.reshape(-1, 16).T, (8, 1))


C, F, S, N, Q = 128, 256, 256, 128, 2
XAV = np.sqrt(6.0 / (F + C))


def sigmoid(v):
    return 1.0 / (1.0 + np.exp(-v))


def setup_inputs():
    return {
        "base": f32(np.random.standard_normal((C, S))),
        "conv": bf(np.random.standard_normal((F, N))),
        "x": bf(np.random.standard_normal((C, N))),
        "h": f32(np.random.standard_normal((C, N))),
        "q": f32(np.random.standard_normal((Q, N))),
        "w_ru": bf(np.random.uniform(-XAV, XAV, (F, Q * F))),
        "b_ru": f32(0.5 * np.random.standard_normal((Q * F, 1))),
        "w_c": bf(np.random.uniform(-XAV, XAV, (C, Q * C))),
        "b_c": f32(0.5 * np.random.standard_normal((Q * C, 1))),
        "offs": striped(np.random.permutation(S)[:N]),
    }


def reference(base, conv, x, h, q, w_ru, b_ru, w_c, b_c, offs):
    idx = offs[:16].T.reshape(-1)
    qq = f64(q)[:, None, :]
    pre = ((f64(w_ru).T @ f64(conv) + f64(b_ru)).reshape(Q, F, N) * qq).sum(axis=0)
    r = sigmoid(pre[:C])
    u = sigmoid(pre[C:])
    cand = np.tanh(((f64(w_c).T @ f64(x) + f64(b_c)).reshape(Q, C, N) * qq).sum(axis=0))
    out = f64(base).copy()
    out[:, idx] = (1.0 - u) * r * f64(h) + u * cand
    return out

@@ -1,0 +1,98 @@
+import concourse.mybir as mybir
+
+F32 = mybir.dt.float32
+BF16 = mybir.dt.bfloat16
+U16 = mybir.dt.uint16
+ALU = mybir.AluOpType
+FUNC = mybir.ActivationFunctionType
+
+P = 128
+N = 128
+S = 256
+D = 2
+KB = 2
+
+FLOPS = 2 * (KB * P) * (D * 2 * P) * N + 2 * P * (D * P) * N
+
+
+def tile_agcrncellwithmlp_kernel(tc, base, conv, x, h, q, w_ru, b_ru, w_c, b_c, offs, out):
+    nc = tc.nc
+    with tc.tile_pool(name="held", bufs=1) as held, tc.psum_pool(name="psum", bufs=1) as psum:
+        offsets = held.tile([P, N // 16], U16, name="offsets")
+        nc.sync.dma_start(offsets[:], offs)
+
+        w_ru_sb = held.tile([P, KB, D * 2 * P], BF16, name="w_ru_sb")
+        nc.sync.dma_start(w_ru_sb[:], w_ru.rearrange("(kb p) e -> p kb e", p=P))
+        conv_sb = held.tile([P, KB, N], BF16, name="conv_sb")
+        nc.scalar.dma_start(conv_sb[:], conv.rearrange("(kb p) j -> p kb j", p=P))
+        w_c_sb = held.tile([P, D * P], BF16, name="w_c_sb")
+        nc.scalar.dma_start(w_c_sb[:], w_c)
+        x_sb = held.tile([P, N], BF16, name="x_sb")
+        nc.scalar.dma_start(x_sb[:], x)
+
+        q_sb = held.tile([P, D * N], F32, name="q_sb")
+        nc.scalar.dma_start(q_sb[:], q.rearrange("d j -> (d j)").partition_broadcast(P))
+
+        b_ru_sb = held.tile([P, D * 2], F32, name="b_ru_sb")
+        b_c_sb = held.tile([P, D], F32, name="b_c_sb")
+        with nc.allow_non_contiguous_dma(reason="a bias vector, one value to a partition"):
+            nc.sync.dma_start(b_ru_sb[:], b_ru.rearrange("(c p) o -> p (c o)", p=P))
+            nc.sync.dma_start(b_c_sb[:], b_c.rearrange("(c p) o -> p (c o)", p=P))
+
+        h_sb = held.tile([P, N], F32, name="h_sb")
+        nc.scalar.dma_start(h_sb[:], h)
+        store = held.tile([P, S], F32, name="store")
+        nc.sync.dma_start(store[:], base)
+
+        def mixed(gate, products, biases):
+            bank = psum.tile([P, D, N], F32, name="bank_" + gate)
+            scaled = held.tile([P, D, N], F32, name="scaled_" + gate)
+            for d in range(D):
+                pairs = products[d]
+                for k, (weights, moving) in enumerate(pairs):
+                    nc.tensor.matmul(
+                        bank[:, d, :], weights, moving, start=(k == 0), stop=(k == len(pairs) - 1)
+                    )
+                nc.vector.scalar_tensor_tensor(
+                    scaled[:, d, :], bank[:, d, :], biases[d], q_sb[:, d * N : (d + 1) * N], ALU.add, ALU.mult
+                )
+            pre = held.tile([P, N], F32, name="pre_" + gate)
+            nc.vector.tensor_tensor(pre[:], scaled[:, 0, :], scaled[:, 1, :], ALU.add)
+            return pre
+
+        def ru_gate(gate, g):
+            products = [
+                [
+                    (w_ru_sb[:, kb, (2 * d + g) * P : (2 * d + g + 1) * P], conv_sb[:, kb, :])
+                    for kb in range(KB)
+                ]
+                for d in range(D)
+            ]
+            return mixed(gate, products, [b_ru_sb[:, 2 * d + g : 2 * d + g + 1] for d in range(D)])
+
+        pre_r = ru_gate("r", 0)
+        pre_u = ru_gate("u", 1)
+        pre_c = mixed(
+            "c",
+            [[(w_c_sb[:, d * P : (d + 1) * P], x_sb[:])] for d in range(D)],
+            [b_c_sb[:, d : d + 1] for d in range(D)],
+        )
+
+        r = held.tile([P, N], F32, name="r")
+        nc.scalar.activation(r[:], pre_r[:], FUNC.Sigmoid)
+        u = held.tile([P, N], F32, name="u")
+        nc.scalar.activation(u[:], pre_u[:], FUNC.Sigmoid)
+        one_minus_u = held.tile([P, N], F32, name="one_minus_u")
+        nc.scalar.activation(one_minus_u[:], pre_u[:], FUNC.Sigmoid, scale=-1.0)
+        cand = held.tile([P, N], F32, name="cand")
+        nc.scalar.activation(cand[:], pre_c[:], FUNC.Tanh)
+
+        r_h = held.tile([P, N], F32, name="r_h")
+        nc.vector.tensor_tensor(r_h[:], r[:], h_sb[:], ALU.mult)
+        kept = held.tile([P, N], F32, name="kept")
+        nc.vector.tensor_tensor(kept[:], one_minus_u[:], r_h[:], ALU.mult)
+        fresh = held.tile([P, N], F32, name="fresh")
+        nc.vector.tensor_tensor(fresh[:], u[:], cand[:], ALU.mult)
+        nc.vector.tensor_tensor(store[:].indirect(offsets[:]), kept[:], fresh[:], ALU.add)
+
+        nc.sync.dma_start(out, store[:])

@@ -18,31 +18,34 @@ FLOPS = 2 * (KB * P) * (D * 2 * P) * N + 2 * P * (D * P) * N
 def tile_agcrncellwithmlp_kernel(tc, base, conv, x, h, q, w_ru, b_ru, w_c, b_c, offs, out):
     nc = tc.nc
     with tc.tile_pool(name="held", bufs=1) as held, tc.psum_pool(name="psum", bufs=1) as psum:
-        offsets = held.tile([P, N // 16], U16, name="offsets")
-        nc.sync.dma_start(offsets[:], offs)
-
-        w_ru_sb = held.tile([P, KB, D * 2 * P], BF16, name="w_ru_sb")
-        nc.sync.dma_start(w_ru_sb[:], w_ru.rearrange("(kb p) e -> p kb e", p=P))
-        conv_sb = held.tile([P, KB, N], BF16, name="conv_sb")
-        nc.scalar.dma_start(conv_sb[:], conv.rearrange("(kb p) j -> p kb j", p=P))
-        w_c_sb = held.tile([P, D * P], BF16, name="w_c_sb")
-        nc.scalar.dma_start(w_c_sb[:], w_c)
         x_sb = held.tile([P, N], BF16, name="x_sb")
-        nc.scalar.dma_start(x_sb[:], x)
-
+        w_c_sb = held.tile([P, D * P], BF16, name="w_c_sb")
         q_sb = held.tile([P, D * N], F32, name="q_sb")
-        nc.scalar.dma_start(q_sb[:], q.rearrange("d j -> (d j)").partition_broadcast(P))
-
-        b_ru_sb = held.tile([P, D * 2], F32, name="b_ru_sb")
         b_c_sb = held.tile([P, D], F32, name="b_c_sb")
+        b_ru_sb = held.tile([P, D * 2], F32, name="b_ru_sb")
+        conv_sb = held.tile([P, KB, N], BF16, name="conv_sb")
+        w_ru_sb = [held.tile([P, D * 2 * P], BF16, name="w_ru_sb" + str(kb)) for kb in range(KB)]
+        h_sb = held.tile([P, N], F32, name="h_sb")
+        offsets = held.tile([P, N // 16], U16, name="offsets")
+        store = held.tile([P, S], F32, name="store")
+
+        nc.sync.dma_start(x_sb[:], x)
+        nc.scalar.dma_start(w_c_sb[:], w_c)
+        nc.sync.dma_start(q_sb[:], q.rearrange("d j -> (d j)").partition_broadcast(P))
+        with nc.allow_non_contiguous_dma(reason="a bias vector, one value to a partition"):
+            nc.scalar.dma_start(b_c_sb[:], b_c.rearrange("(c p) o -> p (c o)", p=P))
+        nc.scalar.dma_start(conv_sb[:], conv.rearrange("(kb p) j -> p kb j", p=P))
+        nc.sync.dma_start(w_ru_sb[0][:], w_ru[0:P, :])
+        nc.scalar.dma_start(w_ru_sb[1][:], w_ru[P : 2 * P, :])
         with nc.allow_non_contiguous_dma(reason="a bias vector, one value to a partition"):
             nc.sync.dma_start(b_ru_sb[:], b_ru.rearrange("(c p) o -> p (c o)", p=P))
-            nc.sync.dma_start(b_c_sb[:], b_c.rearrange("(c p) o -> p (c o)", p=P))
-
-        h_sb = held.tile([P, N], F32, name="h_sb")
-        nc.scalar.dma_start(h_sb[:], h)
-        store = held.tile([P, S], F32, name="store")
+        nc.gpsimd.dma_start(h_sb[:], h)
+        nc.sync.dma_start(offsets[:], offs)
         nc.sync.dma_start(store[:], base)
+
+        dummy = held.tile([P, 1], F32, name="dummy")
+        nc.vector.memset(dummy[:], 0.0)
+        nc.scalar.activation(dummy[:], dummy[:], FUNC.Sigmoid)
 
         def mixed(gate, products, biases):
             bank = psum.tile([P, D, N], F32, name="bank_" + gate)
@@ -62,37 +65,35 @@ def tile_agcrncellwithmlp_kernel(tc, base, conv, x, h, q, w_ru, b_ru, w_c, b_c, 
 
         def ru_gate(gate, g):
             products = [
-                [
-                    (w_ru_sb[:, kb, (2 * d + g) * P : (2 * d + g + 1) * P], conv_sb[:, kb, :])
-                    for kb in range(KB)
-                ]
+                [(w_ru_sb[kb][:, (2 * d + g) * P : (2 * d + g + 1) * P], conv_sb[:, kb, :]) for kb in range(KB)]
                 for d in range(D)
             ]
             return mixed(gate, products, [b_ru_sb[:, 2 * d + g : 2 * d + g + 1] for d in range(D)])
 
-        pre_r = ru_gate("r", 0)
-        pre_u = ru_gate("u", 1)
         pre_c = mixed(
             "c",
             [[(w_c_sb[:, d * P : (d + 1) * P], x_sb[:])] for d in range(D)],
             [b_c_sb[:, d : d + 1] for d in range(D)],
         )
-
-        r = held.tile([P, N], F32, name="r")
-        nc.scalar.activation(r[:], pre_r[:], FUNC.Sigmoid)
-        u = held.tile([P, N], F32, name="u")
-        nc.scalar.activation(u[:], pre_u[:], FUNC.Sigmoid)
-        one_minus_u = held.tile([P, N], F32, name="one_minus_u")
-        nc.scalar.activation(one_minus_u[:], pre_u[:], FUNC.Sigmoid, scale=-1.0)
         cand = held.tile([P, N], F32, name="cand")
         nc.scalar.activation(cand[:], pre_c[:], FUNC.Tanh)
 
-        r_h = held.tile([P, N], F32, name="r_h")
-        nc.vector.tensor_tensor(r_h[:], r[:], h_sb[:], ALU.mult)
-        kept = held.tile([P, N], F32, name="kept")
-        nc.vector.tensor_tensor(kept[:], one_minus_u[:], r_h[:], ALU.mult)
+        pre_u = ru_gate("u", 1)
+        one_minus_u = held.tile([P, N], F32, name="one_minus_u")
+        nc.scalar.activation(one_minus_u[:], pre_u[:], FUNC.Sigmoid, scale=-1.0)
+        u = held.tile([P, N], F32, name="u")
+        nc.scalar.activation(u[:], pre_u[:], FUNC.Sigmoid)
+
+        pre_r = ru_gate("r", 0)
+        r = held.tile([P, N], F32, name="r")
+        nc.scalar.activation(r[:], pre_r[:], FUNC.Sigmoid)
+
+        kept_h = held.tile([P, N], F32, name="kept_h")
+        nc.vector.tensor_tensor(kept_h[:], one_minus_u[:], h_sb[:], ALU.mult)
         fresh = held.tile([P, N], F32, name="fresh")
         nc.vector.tensor_tensor(fresh[:], u[:], cand[:], ALU.mult)
+        kept = held.tile([P, N], F32, name="kept")
+        nc.vector.tensor_tensor(kept[:], kept_h[:], r[:], ALU.mult)
         nc.vector.tensor_tensor(store[:].indirect(offsets[:]), kept[:], fresh[:], ALU.add)
 
         nc.sync.dma_start(out, store[:])

@@ -1,4 +1,5 @@
 import concourse.mybir as mybir
+from concourse.masks import make_identity
 
 F32 = mybir.dt.float32
 BF16 = mybir.dt.bfloat16
@@ -18,34 +19,38 @@ FLOPS = 2 * (KB * P) * (D * 2 * P) * N + 2 * P * (D * P) * N
 def tile_agcrncellwithmlp_kernel(tc, base, conv, x, h, q, w_ru, b_ru, w_c, b_c, offs, out):
     nc = tc.nc
     with tc.tile_pool(name="held", bufs=1) as held, tc.psum_pool(name="psum", bufs=1) as psum:
-        x_sb = held.tile([P, N], BF16, name="x_sb")
-        w_c_sb = held.tile([P, D * P], BF16, name="w_c_sb")
-        q_sb = held.tile([P, D * N], F32, name="q_sb")
-        b_c_sb = held.tile([P, D], F32, name="b_c_sb")
-        b_ru_sb = held.tile([P, D * 2], F32, name="b_ru_sb")
-        conv_sb = held.tile([P, KB, N], BF16, name="conv_sb")
-        w_ru_sb = [held.tile([P, D * 2 * P], BF16, name="w_ru_sb" + str(kb)) for kb in range(KB)]
-        h_sb = held.tile([P, N], F32, name="h_sb")
         offsets = held.tile([P, N // 16], U16, name="offsets")
-        store = held.tile([P, S], F32, name="store")
-
-        nc.sync.dma_start(x_sb[:], x)
-        nc.scalar.dma_start(w_c_sb[:], w_c)
-        nc.sync.dma_start(q_sb[:], q.rearrange("d j -> (d j)").partition_broadcast(P))
-        with nc.allow_non_contiguous_dma(reason="a bias vector, one value to a partition"):
-            nc.scalar.dma_start(b_c_sb[:], b_c.rearrange("(c p) o -> p (c o)", p=P))
-        nc.scalar.dma_start(conv_sb[:], conv.rearrange("(kb p) j -> p kb j", p=P))
-        nc.sync.dma_start(w_ru_sb[0][:], w_ru[0:P, :])
-        nc.scalar.dma_start(w_ru_sb[1][:], w_ru[P : 2 * P, :])
-        with nc.allow_non_contiguous_dma(reason="a bias vector, one value to a partition"):
-            nc.sync.dma_start(b_ru_sb[:], b_ru.rearrange("(c p) o -> p (c o)", p=P))
-        nc.gpsimd.dma_start(h_sb[:], h)
         nc.sync.dma_start(offsets[:], offs)
+
+        w_ru_sb = held.tile([P, KB, D * 2 * P], BF16, name="w_ru_sb")
+        nc.sync.dma_start(w_ru_sb[:], w_ru.rearrange("(kb p) e -> p kb e", p=P))
+        conv_sb = held.tile([P, KB, N], BF16, name="conv_sb")
+        nc.scalar.dma_start(conv_sb[:], conv.rearrange("(kb p) j -> p kb j", p=P))
+        w_c_sb = held.tile([P, D * P], BF16, name="w_c_sb")
+        nc.scalar.dma_start(w_c_sb[:], w_c)
+        x_sb = held.tile([P, N], BF16, name="x_sb")
+        nc.scalar.dma_start(x_sb[:], x)
+
+        q_sb = held.tile([P, D * N], F32, name="q_sb")
+        nc.scalar.dma_start(q_sb[:], q.rearrange("d j -> (d j)").partition_broadcast(P))
+
+        b_ru_rows = held.tile([D * 2, P], F32, name="b_ru_rows")
+        nc.sync.dma_start(b_ru_rows[:], b_ru.rearrange("(c p) o -> c (p o)", p=P))
+        b_c_rows = held.tile([D, P], F32, name="b_c_rows")
+        nc.sync.dma_start(b_c_rows[:], b_c.rearrange("(c p) o -> c (p o)", p=P))
+
+        h_sb = held.tile([P, N], F32, name="h_sb")
+        nc.scalar.dma_start(h_sb[:], h)
+        store = held.tile([P, S], F32, name="store")
         nc.sync.dma_start(store[:], base)
 
-        dummy = held.tile([P, 1], F32, name="dummy")
-        nc.vector.memset(dummy[:], 0.0)
-        nc.scalar.activation(dummy[:], dummy[:], FUNC.Sigmoid)
+        identity = held.tile([D * 2, D * 2], F32, name="identity")
+        make_identity(nc, identity[:])
+        bias_bank = psum.tile([P, D * 3], F32, name="bias_bank")
+        nc.tensor.matmul(bias_bank[:, 0 : D * 2], b_ru_rows[:], identity[:], start=True, stop=True)
+        nc.tensor.matmul(bias_bank[:, D * 2 : D * 3], b_c_rows[:], identity[0:D, 0:D], start=True, stop=True)
+        biases = held.tile([P, D * 3], F32, name="biases")
+        nc.vector.tensor_copy(biases[:], bias_bank[:])
 
         def mixed(gate, products, biases):
             bank = psum.tile([P, D, N], F32, name="bank_" + gate)
@@ -65,35 +70,37 @@ def tile_agcrncellwithmlp_kernel(tc, base, conv, x, h, q, w_ru, b_ru, w_c, b_c, 
 
         def ru_gate(gate, g):
             products = [
-                [(w_ru_sb[kb][:, (2 * d + g) * P : (2 * d + g + 1) * P], conv_sb[:, kb, :]) for kb in range(KB)]
+                [
+                    (w_ru_sb[:, kb, (2 * d + g) * P : (2 * d + g + 1) * P], conv_sb[:, kb, :])
+                    for kb in range(KB)
+                ]
                 for d in range(D)
             ]
-            return mixed(gate, products, [b_ru_sb[:, 2 * d + g : 2 * d + g + 1] for d in range(D)])
+            return mixed(gate, products, [biases[:, 2 * d + g : 2 * d + g + 1] for d in range(D)])
 
+        pre_r = ru_gate("r", 0)
+        pre_u = ru_gate("u", 1)
         pre_c = mixed(
             "c",
             [[(w_c_sb[:, d * P : (d + 1) * P], x_sb[:])] for d in range(D)],
-            [b_c_sb[:, d : d + 1] for d in range(D)],
+            [biases[:, 2 * D + d : 2 * D + d + 1] for d in range(D)],
         )
+
+        r = held.tile([P, N], F32, name="r")
+        nc.scalar.activation(r[:], pre_r[:], FUNC.Sigmoid)
+        u = held.tile([P, N], F32, name="u")
+        nc.scalar.activation(u[:], pre_u[:], FUNC.Sigmoid)
+        one_minus_u = held.tile([P, N], F32, name="one_minus_u")
+        nc.scalar.activation(one_minus_u[:], pre_u[:], FUNC.Sigmoid, scale=-1.0)
         cand = held.tile([P, N], F32, name="cand")
         nc.scalar.activation(cand[:], pre_c[:], FUNC.Tanh)
 
-        pre_u = ru_gate("u", 1)
-        one_minus_u = held.tile([P, N], F32, name="one_minus_u")
-        nc.scalar.activation(one_minus_u[:], pre_u[:], FUNC.Sigmoid, scale=-1.0)
-        u = held.tile([P, N], F32, name="u")
-        nc.scalar.activation(u[:], pre_u[:], FUNC.Sigmoid)
-
-        pre_r = ru_gate("r", 0)
-        r = held.tile([P, N], F32, name="r")
-        nc.scalar.activation(r[:], pre_r[:], FUNC.Sigmoid)
-
-        kept_h = held.tile([P, N], F32, name="kept_h")
-        nc.vector.tensor_tensor(kept_h[:], one_minus_u[:], h_sb[:], ALU.mult)
+        r_h = held.tile([P, N], F32, name="r_h")
+        nc.vector.tensor_tensor(r_h[:], r[:], h_sb[:], ALU.mult)
+        kept = held.tile([P, N], F32, name="kept")
+        nc.vector.tensor_tensor(kept[:], one_minus_u[:], r_h[:], ALU.mult)
         fresh = held.tile([P, N], F32, name="fresh")
         nc.vector.tensor_tensor(fresh[:], u[:], cand[:], ALU.mult)
-        kept = held.tile([P, N], F32, name="kept")
-        nc.vector.tensor_tensor(kept[:], kept_h[:], r[:], ALU.mult)
         nc.vector.tensor_tensor(store[:].indirect(offsets[:]), kept[:], fresh[:], ALU.add)
 
         nc.sync.dma_start(out, store[:])

@@ -19,30 +19,31 @@ FLOPS = 2 * (KB * P) * (D * 2 * P) * N + 2 * P * (D * P) * N
 def tile_agcrncellwithmlp_kernel(tc, base, conv, x, h, q, w_ru, b_ru, w_c, b_c, offs, out):
     nc = tc.nc
     with tc.tile_pool(name="held", bufs=1) as held, tc.psum_pool(name="psum", bufs=1) as psum:
-        offsets = held.tile([P, N // 16], U16, name="offsets")
-        nc.sync.dma_start(offsets[:], offs)
-
-        w_ru_sb = held.tile([P, KB, D * 2 * P], BF16, name="w_ru_sb")
-        nc.sync.dma_start(w_ru_sb[:], w_ru.rearrange("(kb p) e -> p kb e", p=P))
-        conv_sb = held.tile([P, KB, N], BF16, name="conv_sb")
-        nc.scalar.dma_start(conv_sb[:], conv.rearrange("(kb p) j -> p kb j", p=P))
-        w_c_sb = held.tile([P, D * P], BF16, name="w_c_sb")
-        nc.scalar.dma_start(w_c_sb[:], w_c)
         x_sb = held.tile([P, N], BF16, name="x_sb")
-        nc.scalar.dma_start(x_sb[:], x)
-
+        w_c_sb = held.tile([P, D * P], BF16, name="w_c_sb")
         q_sb = held.tile([P, D * N], F32, name="q_sb")
-        nc.scalar.dma_start(q_sb[:], q.rearrange("d j -> (d j)").partition_broadcast(P))
-
-        b_ru_rows = held.tile([D * 2, P], F32, name="b_ru_rows")
-        nc.sync.dma_start(b_ru_rows[:], b_ru.rearrange("(c p) o -> c (p o)", p=P))
         b_c_rows = held.tile([D, P], F32, name="b_c_rows")
-        nc.sync.dma_start(b_c_rows[:], b_c.rearrange("(c p) o -> c (p o)", p=P))
-
+        b_ru_rows = held.tile([D * 2, P], F32, name="b_ru_rows")
+        conv_sb = held.tile([P, KB, N], BF16, name="conv_sb")
+        w_ru_sb = held.tile([P, KB, D * 2 * P], BF16, name="w_ru_sb")
         h_sb = held.tile([P, N], F32, name="h_sb")
-        nc.scalar.dma_start(h_sb[:], h)
+        offsets = held.tile([P, N // 16], U16, name="offsets")
         store = held.tile([P, S], F32, name="store")
+
+        nc.sync.dma_start(x_sb[:], x)
+        nc.scalar.dma_start(w_c_sb[:], w_c)
+        nc.sync.dma_start(b_c_rows[:], b_c.rearrange("(c p) o -> c (p o)", p=P))
+        nc.scalar.dma_start(q_sb[:], q.rearrange("d j -> (d j)").partition_broadcast(P))
+        nc.sync.dma_start(w_ru_sb[:], w_ru.rearrange("(kb p) e -> p kb e", p=P))
+        nc.scalar.dma_start(conv_sb[:], conv.rearrange("(kb p) j -> p kb j", p=P))
+        nc.scalar.dma_start(b_ru_rows[:], b_ru.rearrange("(c p) o -> c (p o)", p=P))
+        nc.sync.dma_start(offsets[:], offs)
+        nc.sync.dma_start(h_sb[:], h)
         nc.sync.dma_start(store[:], base)
+
+        dummy = held.tile([P, 1], F32, name="dummy")
+        nc.gpsimd.memset(dummy[:], 0.0)
+        nc.scalar.activation(dummy[:], dummy[:], FUNC.Sigmoid)
 
         identity = held.tile([D * 2, D * 2], F32, name="identity")
         make_identity(nc, identity[:])
@@ -52,7 +53,7 @@ def tile_agcrncellwithmlp_kernel(tc, base, conv, x, h, q, w_ru, b_ru, w_c, b_c, 
         biases = held.tile([P, D * 3], F32, name="biases")
         nc.vector.tensor_copy(biases[:], bias_bank[:])
 
-        def mixed(gate, products, biases):
+        def mixed(gate, products, gate_biases):
             bank = psum.tile([P, D, N], F32, name="bank_" + gate)
             scaled = held.tile([P, D, N], F32, name="scaled_" + gate)
             for d in range(D):
@@ -62,7 +63,7 @@ def tile_agcrncellwithmlp_kernel(tc, base, conv, x, h, q, w_ru, b_ru, w_c, b_c, 
                         bank[:, d, :], weights, moving, start=(k == 0), stop=(k == len(pairs) - 1)
                     )
                 nc.vector.scalar_tensor_tensor(
-                    scaled[:, d, :], bank[:, d, :], biases[d], q_sb[:, d * N : (d + 1) * N], ALU.add, ALU.mult
+                    scaled[:, d, :], bank[:, d, :], gate_biases[d], q_sb[:, d * N : (d + 1) * N], ALU.add, ALU.mult
                 )
             pre = held.tile([P, N], F32, name="pre_" + gate)
             nc.vector.tensor_tensor(pre[:], scaled[:, 0, :], scaled[:, 1, :], ALU.add)
@@ -70,37 +71,35 @@ def tile_agcrncellwithmlp_kernel(tc, base, conv, x, h, q, w_ru, b_ru, w_c, b_c, 
 
         def ru_gate(gate, g):
             products = [
-                [
-                    (w_ru_sb[:, kb, (2 * d + g) * P : (2 * d + g + 1) * P], conv_sb[:, kb, :])
-                    for kb in range(KB)
-                ]
+                [(w_ru_sb[:, kb, (2 * d + g) * P : (2 * d + g + 1) * P], conv_sb[:, kb, :]) for kb in range(KB)]
                 for d in range(D)
             ]
             return mixed(gate, products, [biases[:, 2 * d + g : 2 * d + g + 1] for d in range(D)])
 
-        pre_r = ru_gate("r", 0)
-        pre_u = ru_gate("u", 1)
         pre_c = mixed(
             "c",
             [[(w_c_sb[:, d * P : (d + 1) * P], x_sb[:])] for d in range(D)],
             [biases[:, 2 * D + d : 2 * D + d + 1] for d in range(D)],
         )
-
-        r = held.tile([P, N], F32, name="r")
-        nc.scalar.activation(r[:], pre_r[:], FUNC.Sigmoid)
-        u = held.tile([P, N], F32, name="u")
-        nc.scalar.activation(u[:], pre_u[:], FUNC.Sigmoid)
-        one_minus_u = held.tile([P, N], F32, name="one_minus_u")
-        nc.scalar.activation(one_minus_u[:], pre_u[:], FUNC.Sigmoid, scale=-1.0)
         cand = held.tile([P, N], F32, name="cand")
         nc.scalar.activation(cand[:], pre_c[:], FUNC.Tanh)
 
-        r_h = held.tile([P, N], F32, name="r_h")
-        nc.vector.tensor_tensor(r_h[:], r[:], h_sb[:], ALU.mult)
-        kept = held.tile([P, N], F32, name="kept")
-        nc.vector.tensor_tensor(kept[:], one_minus_u[:], r_h[:], ALU.mult)
+        pre_u = ru_gate("u", 1)
+        one_minus_u = held.tile([P, N], F32, name="one_minus_u")
+        nc.scalar.activation(one_minus_u[:], pre_u[:], FUNC.Sigmoid, scale=-1.0)
+        u = held.tile([P, N], F32, name="u")
+        nc.scalar.activation(u[:], pre_u[:], FUNC.Sigmoid)
+
+        pre_r = ru_gate("r", 0)
+        r = held.tile([P, N], F32, name="r")
+        nc.scalar.activation(r[:], pre_r[:], FUNC.Sigmoid)
+
+        kept_h = held.tile([P, N], F32, name="kept_h")
+        nc.vector.tensor_tensor(kept_h[:], one_minus_u[:], h_sb[:], ALU.mult)
         fresh = held.tile([P, N], F32, name="fresh")
         nc.vector.tensor_tensor(fresh[:], u[:], cand[:], ALU.mult)
+        kept = held.tile([P, N], F32, name="kept")
+        nc.vector.tensor_tensor(kept[:], kept_h[:], r[:], ALU.mult)
         nc.vector.tensor_tensor(store[:].indirect(offsets[:]), kept[:], fresh[:], ALU.add)
 
         nc.sync.dma_start(out, store[:])

@@ -32,17 +32,17 @@ def tile_agcrncellwithmlp_kernel(tc, base, conv, x, h, q, w_ru, b_ru, w_c, b_c, 
 
         nc.sync.dma_start(x_sb[:], x)
         nc.scalar.dma_start(w_c_sb[:], w_c)
-        nc.sync.dma_start(b_c_rows[:], b_c.rearrange("(c p) o -> c (p o)", p=P))
         nc.scalar.dma_start(q_sb[:], q.rearrange("d j -> (d j)").partition_broadcast(P))
+        nc.sync.dma_start(b_c_rows[:], b_c.rearrange("(c p) o -> c (p o)", p=P))
+        nc.sync.dma_start(b_ru_rows[:], b_ru.rearrange("(c p) o -> c (p o)", p=P))
         nc.sync.dma_start(w_ru_sb[:], w_ru.rearrange("(kb p) e -> p kb e", p=P))
-        nc.scalar.dma_start(conv_sb[:], conv.rearrange("(kb p) j -> p kb j", p=P))
-        nc.scalar.dma_start(b_ru_rows[:], b_ru.rearrange("(c p) o -> c (p o)", p=P))
+        nc.sync.dma_start(conv_sb[:], conv.rearrange("(kb p) j -> p kb j", p=P))
         nc.sync.dma_start(offsets[:], offs)
         nc.sync.dma_start(h_sb[:], h)
         nc.sync.dma_start(store[:], base)
 
         dummy = held.tile([P, 1], F32, name="dummy")
-        nc.gpsimd.memset(dummy[:], 0.0)
+        nc.vector.memset(dummy[:], 0.0)
         nc.scalar.activation(dummy[:], dummy[:], FUNC.Sigmoid)
 
         identity = held.tile([D * 2, D * 2], F32, name="identity")

@@ -1,5 +1,4 @@
 import concourse.mybir as mybir
-from concourse.masks import make_identity
 
 F32 = mybir.dt.float32
 BF16 = mybir.dt.bfloat16
@@ -19,51 +18,51 @@ FLOPS = 2 * (KB * P) * (D * 2 * P) * N + 2 * P * (D * P) * N
 def tile_agcrncellwithmlp_kernel(tc, base, conv, x, h, q, w_ru, b_ru, w_c, b_c, offs, out):
     nc = tc.nc
     with tc.tile_pool(name="held", bufs=1) as held, tc.psum_pool(name="psum", bufs=1) as psum:
-        x_sb = held.tile([P, N], BF16, name="x_sb")
-        w_c_sb = held.tile([P, D * P], BF16, name="w_c_sb")
-        q_sb = held.tile([P, D * N], F32, name="q_sb")
-        b_c_rows = held.tile([D, P], F32, name="b_c_rows")
-        b_ru_rows = held.tile([D * 2, P], F32, name="b_ru_rows")
-        conv_sb = held.tile([P, KB, N], BF16, name="conv_sb")
-        w_ru_sb = held.tile([P, KB, D * 2 * P], BF16, name="w_ru_sb")
-        h_sb = held.tile([P, N], F32, name="h_sb")
         offsets = held.tile([P, N // 16], U16, name="offsets")
+        w_ru_sb = held.tile([P, KB, D * 2 * P], BF16, name="w_ru_sb")
+        conv_sb = held.tile([P, KB, N], BF16, name="conv_sb")
+        q_sb = held.tile([P, D * N], F32, name="q_sb")
+        b_ru_rows = held.tile([D * 2, P], F32, name="b_ru_rows")
+        b_c_rows = held.tile([D, P], F32, name="b_c_rows")
+        w_c_sb = held.tile([P, D * P], BF16, name="w_c_sb")
+        x_sb = held.tile([P, N], BF16, name="x_sb")
+        h_sb = held.tile([P, N], F32, name="h_sb")
         store = held.tile([P, S], F32, name="store")
 
-        nc.sync.dma_start(x_sb[:], x)
-        nc.scalar.dma_start(w_c_sb[:], w_c)
-        nc.scalar.dma_start(q_sb[:], q.rearrange("d j -> (d j)").partition_broadcast(P))
-        nc.sync.dma_start(b_c_rows[:], b_c.rearrange("(c p) o -> c (p o)", p=P))
-        nc.sync.dma_start(b_ru_rows[:], b_ru.rearrange("(c p) o -> c (p o)", p=P))
+        nc.scalar.dma_start(b_ru_rows[:], b_ru.rearrange("(c p) o -> c (p o)", p=P))
         nc.sync.dma_start(w_ru_sb[:], w_ru.rearrange("(kb p) e -> p kb e", p=P))
+        nc.scalar.dma_start(b_c_rows[:], b_c.rearrange("(c p) o -> c (p o)", p=P))
         nc.sync.dma_start(conv_sb[:], conv.rearrange("(kb p) j -> p kb j", p=P))
+        nc.scalar.dma_start(w_c_sb[:], w_c)
+        nc.sync.dma_start(q_sb[:], q.rearrange("d j -> (d j)").partition_broadcast(P))
+        nc.scalar.dma_start(x_sb[:], x)
         nc.sync.dma_start(offsets[:], offs)
-        nc.sync.dma_start(h_sb[:], h)
+        nc.scalar.dma_start(h_sb[:], h)
         nc.sync.dma_start(store[:], base)
 
-        dummy = held.tile([P, 1], F32, name="dummy")
-        nc.vector.memset(dummy[:], 0.0)
-        nc.scalar.activation(dummy[:], dummy[:], FUNC.Sigmoid)
-
         identity = held.tile([D * 2, D * 2], F32, name="identity")
-        make_identity(nc, identity[:])
-        bias_bank = psum.tile([P, D * 3], F32, name="bias_bank")
-        nc.tensor.matmul(bias_bank[:, 0 : D * 2], b_ru_rows[:], identity[:], start=True, stop=True)
-        nc.tensor.matmul(bias_bank[:, D * 2 : D * 3], b_c_rows[:], identity[0:D, 0:D], start=True, stop=True)
-        biases = held.tile([P, D * 3], F32, name="biases")
-        nc.vector.tensor_copy(biases[:], bias_bank[:])
+        nc.vector.memset(identity[:], 0.0)
+        for k in range(D * 2):
+            nc.vector.memset(identity[0 : k + 1, k : k + 1], 1.0)
+        for k in range(1, D * 2):
+            nc.vector.memset(identity[0:k, k : k + 1], 0.0)
+
+        def as_columns(rows, count, name):
+            bank = psum.tile([P, count], F32, name="bank_" + name)
+            nc.tensor.matmul(bank[:], rows[:], identity[0:count, 0:count], start=True, stop=True)
+            columns = held.tile([P, count], F32, name=name)
+            nc.vector.tensor_copy(columns[:], bank[:])
+            return columns
 
         def mixed(gate, products, gate_biases):
-            bank = psum.tile([P, D, N], F32, name="bank_" + gate)
             scaled = held.tile([P, D, N], F32, name="scaled_" + gate)
             for d in range(D):
+                bank = psum.tile([P, N], F32, name="bank_" + gate + str(d))
                 pairs = products[d]
                 for k, (weights, moving) in enumerate(pairs):
-                    nc.tensor.matmul(
-                        bank[:, d, :], weights, moving, start=(k == 0), stop=(k == len(pairs) - 1)
-                    )
+                    nc.tensor.matmul(bank[:], weights, moving, start=(k == 0), stop=(k == len(pairs) - 1))
                 nc.vector.scalar_tensor_tensor(
-                    scaled[:, d, :], bank[:, d, :], gate_biases[d], q_sb[:, d * N : (d + 1) * N], ALU.add, ALU.mult
+                    scaled[:, d, :], bank[:], gate_biases[d], q_sb[:, d * N : (d + 1) * N], ALU.add, ALU.mult
                 )
             pre = held.tile([P, N], F32, name="pre_" + gate)
             nc.vector.tensor_tensor(pre[:], scaled[:, 0, :], scaled[:, 1, :], ALU.add)
@@ -74,15 +73,12 @@ def tile_agcrncellwithmlp_kernel(tc, base, conv, x, h, q, w_ru, b_ru, w_c, b_c, 
                 [(w_ru_sb[:, kb, (2 * d + g) * P : (2 * d + g + 1) * P], conv_sb[:, kb, :]) for kb in range(KB)]
                 for d in range(D)
             ]
-            return mixed(gate, products, [biases[:, 2 * d + g : 2 * d + g + 1] for d in range(D)])
+            return mixed(gate, products, [b_ru_sb[:, 2 * d + g : 2 * d + g + 1] for d in range(D)])
 
-        pre_c = mixed(
-            "c",
-            [[(w_c_sb[:, d * P : (d + 1) * P], x_sb[:])] for d in range(D)],
-            [biases[:, 2 * D + d : 2 * D + d + 1] for d in range(D)],
-        )
-        cand = held.tile([P, N], F32, name="cand")
-        nc.scalar.activation(cand[:], pre_c[:], FUNC.Tanh)
+        b_ru_sb = as_columns(b_ru_rows, D * 2, "b_ru_sb")
+        pre_r = ru_gate("r", 0)
+        r = held.tile([P, N], F32, name="r")
+        nc.scalar.activation(r[:], pre_r[:], FUNC.Sigmoid)
 
         pre_u = ru_gate("u", 1)
         one_minus_u = held.tile([P, N], F32, name="one_minus_u")
@@ -90,16 +86,21 @@ def tile_agcrncellwithmlp_kernel(tc, base, conv, x, h, q, w_ru, b_ru, w_c, b_c, 
         u = held.tile([P, N], F32, name="u")
         nc.scalar.activation(u[:], pre_u[:], FUNC.Sigmoid)
 
-        pre_r = ru_gate("r", 0)
-        r = held.tile([P, N], F32, name="r")
-        nc.scalar.activation(r[:], pre_r[:], FUNC.Sigmoid)
+        b_c_sb = as_columns(b_c_rows, D, "b_c_sb")
+        pre_c = mixed(
+            "c",
+            [[(w_c_sb[:, d * P : (d + 1) * P], x_sb[:])] for d in range(D)],
+            [b_c_sb[:, d : d + 1] for d in range(D)],
+        )
+        cand = held.tile([P, N], F32, name="cand")
+        nc.scalar.activation(cand[:], pre_c[:], FUNC.Tanh)
 
-        kept_h = held.tile([P, N], F32, name="kept_h")
-        nc.vector.tensor_tensor(kept_h[:], one_minus_u[:], h_sb[:], ALU.mult)
+        r_h = held.tile([P, N], F32, name="r_h")
+        nc.vector.tensor_tensor(r_h[:], r[:], h_sb[:], ALU.mult)
+        kept = held.tile([P, N], F32, name="kept")
+        nc.vector.tensor_tensor(kept[:], one_minus_u[:], r_h[:], ALU.mult)
         fresh = held.tile([P, N], F32, name="fresh")
         nc.vector.tensor_tensor(fresh[:], u[:], cand[:], ALU.mult)
-        kept = held.tile([P, N], F32, name="kept")
-        nc.vector.tensor_tensor(kept[:], kept_h[:], r[:], ALU.mult)
         nc.vector.tensor_tensor(store[:].indirect(offsets[:]), kept[:], fresh[:], ALU.add)
 
         nc.sync.dma_start(out, store[:])

@@ -21,7 +21,7 @@ def tile_agcrncellwithmlp_kernel(tc, base, conv, x, h, q, w_ru, b_ru, w_c, b_c, 
         offsets = held.tile([P, N // 16], U16, name="offsets")
         w_ru_sb = held.tile([P, KB, D * 2 * P], BF16, name="w_ru_sb")
         conv_sb = held.tile([P, KB, N], BF16, name="conv_sb")
-        q_sb = held.tile([P, D * N], F32, name="q_sb")
+        q_row = held.tile([1, D * N], F32, name="q_row")
         b_ru_rows = held.tile([D * 2, P], F32, name="b_ru_rows")
         b_c_rows = held.tile([D, P], F32, name="b_c_rows")
         w_c_sb = held.tile([P, D * P], BF16, name="w_c_sb")
@@ -29,17 +29,19 @@ def tile_agcrncellwithmlp_kernel(tc, base, conv, x, h, q, w_ru, b_ru, w_c, b_c, 
         h_sb = held.tile([P, N], F32, name="h_sb")
         store = held.tile([P, S], F32, name="store")
 
+        nc.scalar.dma_start(q_row[:], q.rearrange("d j -> (d j)").unsqueeze(0))
+        nc.sync.dma_start(offsets[:], offs)
         nc.scalar.dma_start(b_ru_rows[:], b_ru.rearrange("(c p) o -> c (p o)", p=P))
         nc.sync.dma_start(w_ru_sb[:], w_ru.rearrange("(kb p) e -> p kb e", p=P))
         nc.scalar.dma_start(b_c_rows[:], b_c.rearrange("(c p) o -> c (p o)", p=P))
         nc.sync.dma_start(conv_sb[:], conv.rearrange("(kb p) j -> p kb j", p=P))
-        nc.scalar.dma_start(w_c_sb[:], w_c)
-        nc.sync.dma_start(q_sb[:], q.rearrange("d j -> (d j)").partition_broadcast(P))
-        nc.scalar.dma_start(x_sb[:], x)
-        nc.sync.dma_start(offsets[:], offs)
+        nc.sync.dma_start(w_c_sb[:], w_c)
+        nc.sync.dma_start(x_sb[:], x)
         nc.scalar.dma_start(h_sb[:], h)
         nc.sync.dma_start(store[:], base)
 
+        ones_row = held.tile([1, P], F32, name="ones_row")
+        nc.vector.memset(ones_row[:], 1.0)
         identity = held.tile([D * 2, D * 2], F32, name="identity")
         nc.vector.memset(identity[:], 0.0)
         for k in range(D * 2):
@@ -47,12 +49,16 @@ def tile_agcrncellwithmlp_kernel(tc, base, conv, x, h, q, w_ru, b_ru, w_c, b_c, 
         for k in range(1, D * 2):
             nc.vector.memset(identity[0:k, k : k + 1], 0.0)
 
-        def as_columns(rows, count, name):
-            bank = psum.tile([P, count], F32, name="bank_" + name)
-            nc.tensor.matmul(bank[:], rows[:], identity[0:count, 0:count], start=True, stop=True)
-            columns = held.tile([P, count], F32, name=name)
-            nc.vector.tensor_copy(columns[:], bank[:])
-            return columns
+        q_bank = psum.tile([P, D * N], F32, name="q_bank")
+        nc.tensor.matmul(q_bank[:], ones_row[:], q_row[:], start=True, stop=True)
+        q_sb = held.tile([P, D * N], F32, name="q_sb")
+        nc.vector.tensor_copy(q_sb[:], q_bank[:])
+
+        bias_bank = psum.tile([P, D * 3], F32, name="bias_bank")
+        nc.tensor.matmul(bias_bank[:, 0 : D * 2], b_ru_rows[:], identity[:], start=True, stop=True)
+        nc.tensor.matmul(bias_bank[:, D * 2 : D * 3], b_c_rows[:], identity[0:D, 0:D], start=True, stop=True)
+        biases = held.tile([P, D * 3], F32, name="biases")
+        nc.vector.tensor_copy(biases[:], bias_bank[:])
 
         def mixed(gate, products, gate_biases):
             scaled = held.tile([P, D, N], F32, name="scaled_" + gate)
@@ -73,9 +79,8 @@ def tile_agcrncellwithmlp_kernel(tc, base, conv, x, h, q, w_ru, b_ru, w_c, b_c, 
                 [(w_ru_sb[:, kb, (2 * d + g) * P : (2 * d + g + 1) * P], conv_sb[:, kb, :]) for kb in range(KB)]
                 for d in range(D)
             ]
-            return mixed(gate, products, [b_ru_sb[:, 2 * d + g : 2 * d + g + 1] for d in range(D)])
+            return mixed(gate, products, [biases[:, 2 * d + g : 2 * d + g + 1] for d in range(D)])
 
-        b_ru_sb = as_columns(b_ru_rows, D * 2, "b_ru_sb")
         pre_r = ru_gate("r", 0)
         r = held.tile([P, N], F32, name="r")
         nc.scalar.activation(r[:], pre_r[:], FUNC.Sigmoid)
@@ -86,11 +91,10 @@ def tile_agcrncellwithmlp_kernel(tc, base, conv, x, h, q, w_ru, b_ru, w_c, b_c, 
         u = held.tile([P, N], F32, name="u")
         nc.scalar.activation(u[:], pre_u[:], FUNC.Sigmoid)
 
-        b_c_sb = as_columns(b_c_rows, D, "b_c_sb")
         pre_c = mixed(
             "c",
             [[(w_c_sb[:, d * P : (d + 1) * P], x_sb[:])] for d in range(D)],
-            [b_c_sb[:, d : d + 1] for d in range(D)],
+            [biases[:, 2 * D + d : 2 * D + d + 1] for d in range(D)],
         )
         cand = held.tile([P, N], F32, name="cand")
         nc.scalar.activation(cand[:], pre_c[:], FUNC.Tanh)

@@ -11,6 +11,7 @@ N = 128
 S = 256
 D = 2
 KB = 2
+WARM_UP_PRODUCTS = 4
 
 FLOPS = 2 * (KB * P) * (D * 2 * P) * N + 2 * P * (D * P) * N
 
@@ -22,8 +23,7 @@ def tile_agcrncellwithmlp_kernel(tc, base, conv, x, h, q, w_ru, b_ru, w_c, b_c, 
         w_ru_sb = held.tile([P, KB, D * 2 * P], BF16, name="w_ru_sb")
         conv_sb = held.tile([P, KB, N], BF16, name="conv_sb")
         q_row = held.tile([1, D * N], F32, name="q_row")
-        b_ru_rows = held.tile([D * 2, P], F32, name="b_ru_rows")
-        b_c_rows = held.tile([D, P], F32, name="b_c_rows")
+        b_rows = held.tile([D * 3, P], F32, name="b_rows")
         w_c_sb = held.tile([P, D * P], BF16, name="w_c_sb")
         x_sb = held.tile([P, N], BF16, name="x_sb")
         h_sb = held.tile([P, N], F32, name="h_sb")
@@ -31,32 +31,36 @@ def tile_agcrncellwithmlp_kernel(tc, base, conv, x, h, q, w_ru, b_ru, w_c, b_c, 
 
         nc.scalar.dma_start(q_row[:], q.rearrange("d j -> (d j)").unsqueeze(0))
         nc.sync.dma_start(offsets[:], offs)
-        nc.scalar.dma_start(b_ru_rows[:], b_ru.rearrange("(c p) o -> c (p o)", p=P))
+        nc.scalar.dma_start(b_rows[0 : D * 2, :], b_ru.rearrange("(c p) o -> c (p o)", p=P))
         nc.sync.dma_start(w_ru_sb[:], w_ru.rearrange("(kb p) e -> p kb e", p=P))
-        nc.scalar.dma_start(b_c_rows[:], b_c.rearrange("(c p) o -> c (p o)", p=P))
+        nc.scalar.dma_start(b_rows[D * 2 : D * 3, :], b_c.rearrange("(c p) o -> c (p o)", p=P))
         nc.sync.dma_start(conv_sb[:], conv.rearrange("(kb p) j -> p kb j", p=P))
         nc.sync.dma_start(w_c_sb[:], w_c)
         nc.sync.dma_start(x_sb[:], x)
         nc.scalar.dma_start(h_sb[:], h)
         nc.sync.dma_start(store[:], base)
 
+        zeros = held.tile([P, D * N], BF16, name="zeros")
+        nc.vector.memset(zeros[:], 0.0)
+        q_bank = psum.tile([P, D * N], F32, name="q_bank")
+        for i in range(WARM_UP_PRODUCTS):
+            nc.tensor.matmul(q_bank[:], zeros[:, 0:P], zeros[:], start=True, stop=True)
+
         ones_row = held.tile([1, P], F32, name="ones_row")
         nc.vector.memset(ones_row[:], 1.0)
-        identity = held.tile([D * 2, D * 2], F32, name="identity")
+        identity = held.tile([D * 3, D * 3], F32, name="identity")
         nc.vector.memset(identity[:], 0.0)
-        for k in range(D * 2):
+        for k in range(D * 3):
             nc.vector.memset(identity[0 : k + 1, k : k + 1], 1.0)
-        for k in range(1, D * 2):
+        for k in range(1, D * 3):
             nc.vector.memset(identity[0:k, k : k + 1], 0.0)
 
-        q_bank = psum.tile([P, D * N], F32, name="q_bank")
         nc.tensor.matmul(q_bank[:], ones_row[:], q_row[:], start=True, stop=True)
         q_sb = held.tile([P, D * N], F32, name="q_sb")
         nc.vector.tensor_copy(q_sb[:], q_bank[:])
 
         bias_bank = psum.tile([P, D * 3], F32, name="bias_bank")
-        nc.tensor.matmul(bias_bank[:, 0 : D * 2], b_ru_rows[:], identity[:], start=True, stop=True)
-        nc.tensor.matmul(bias_bank[:, D * 2 : D * 3], b_c_rows[:], identity[0:D, 0:D], start=True, stop=True)
+        nc.tensor.matmul(bias_bank[:], b_rows[:], identity[:], start=True, stop=True)
         biases = held.tile([P, D * 3], F32, name="biases")
         nc.vector.tensor_copy(biases[:], bias_bank[:])
 

@@ -29,16 +29,16 @@ def tile_agcrncellwithmlp_kernel(tc, base, conv, x, h, q, w_ru, b_ru, w_c, b_c, 
         h_sb = held.tile([P, N], F32, name="h_sb")
         store = held.tile([P, S], F32, name="store")
 
-        nc.scalar.dma_start(q_row[:], q.rearrange("d j -> (d j)").unsqueeze(0))
-        nc.sync.dma_start(offsets[:], offs)
+        nc.sync.dma_start(q_row[:], q.rearrange("d j -> (d j)").unsqueeze(0))
         nc.scalar.dma_start(b_rows[0 : D * 2, :], b_ru.rearrange("(c p) o -> c (p o)", p=P))
         nc.sync.dma_start(w_ru_sb[:], w_ru.rearrange("(kb p) e -> p kb e", p=P))
         nc.scalar.dma_start(b_rows[D * 2 : D * 3, :], b_c.rearrange("(c p) o -> c (p o)", p=P))
         nc.sync.dma_start(conv_sb[:], conv.rearrange("(kb p) j -> p kb j", p=P))
+        nc.scalar.dma_start(h_sb[:], h)
         nc.sync.dma_start(w_c_sb[:], w_c)
         nc.sync.dma_start(x_sb[:], x)
-        nc.scalar.dma_start(h_sb[:], h)
         nc.sync.dma_start(store[:], base)
+        nc.sync.dma_start(offsets[:], offs)
 
         zeros = held.tile([P, D * N], BF16, name="zeros")
         nc.vector.memset(zeros[:], 0.0)

@@ -20,7 +20,7 @@ def tile_agcrncellwithmlp_kernel(tc, base, conv, x, h, q, w_ru, b_ru, w_c, b_c, 
     nc = tc.nc
     with tc.tile_pool(name="held", bufs=1) as held, tc.psum_pool(name="psum", bufs=1) as psum:
         offsets = held.tile([P, N // 16], U16, name="offsets")
-        w_ru_sb = held.tile([P, KB, D * 2 * P], BF16, name="w_ru_sb")
+        w_ru_sb = [held.tile([P, KB, 2 * P], BF16, name="w_ru_sb%d" % d) for d in range(D)]
         conv_sb = held.tile([P, KB, N], BF16, name="conv_sb")
         q_row = held.tile([1, D * N], F32, name="q_row")
         b_rows = held.tile([D * 3, P], F32, name="b_rows")
@@ -29,11 +29,13 @@ def tile_agcrncellwithmlp_kernel(tc, base, conv, x, h, q, w_ru, b_ru, w_c, b_c, 
         h_sb = held.tile([P, N], F32, name="h_sb")
         store = held.tile([P, S], F32, name="store")
 
+        w_ru_blocks = w_ru.rearrange("(kb p) e -> p kb e", p=P)
         nc.sync.dma_start(q_row[:], q.rearrange("d j -> (d j)").unsqueeze(0))
         nc.scalar.dma_start(b_rows[0 : D * 2, :], b_ru.rearrange("(c p) o -> c (p o)", p=P))
-        nc.sync.dma_start(w_ru_sb[:], w_ru.rearrange("(kb p) e -> p kb e", p=P))
+        nc.sync.dma_start(w_ru_sb[0][:], w_ru_blocks[:, :, 0 : 2 * P])
         nc.scalar.dma_start(b_rows[D * 2 : D * 3, :], b_c.rearrange("(c p) o -> c (p o)", p=P))
-        nc.sync.dma_start(conv_sb[:], conv.rearrange("(kb p) j -> p kb j", p=P))
+        nc.sync.dma_start(w_ru_sb[1][:], w_ru_blocks[:, :, 2 * P : 4 * P])
+        nc.scalar.dma_start(conv_sb[:], conv.rearrange("(kb p) j -> p kb j", p=P))
         nc.scalar.dma_start(h_sb[:], h)
         nc.sync.dma_start(w_c_sb[:], w_c)
         nc.sync.dma_start(x_sb[:], x)
@@ -64,42 +66,47 @@ def tile_agcrncellwithmlp_kernel(tc, base, conv, x, h, q, w_ru, b_ru, w_c, b_c, 
         biases = held.tile([P, D * 3], F32, name="biases")
         nc.vector.tensor_copy(biases[:], bias_bank[:])
 
-        def mixed(gate, products, gate_biases):
-            scaled = held.tile([P, D, N], F32, name="scaled_" + gate)
-            for d in range(D):
-                bank = psum.tile([P, N], F32, name="bank_" + gate + str(d))
-                pairs = products[d]
-                for k, (weights, moving) in enumerate(pairs):
-                    nc.tensor.matmul(bank[:], weights, moving, start=(k == 0), stop=(k == len(pairs) - 1))
-                nc.vector.scalar_tensor_tensor(
-                    scaled[:, d, :], bank[:], gate_biases[d], q_sb[:, d * N : (d + 1) * N], ALU.add, ALU.mult
-                )
+        scaled = {}
+        for gate in ("r", "u", "c"):
+            scaled[gate] = held.tile([P, D, N], F32, name="scaled_" + gate)
+
+        def product_and_scaling(gate, d, pairs, bias):
+            bank = psum.tile([P, N], F32, name="bank_%s%d" % (gate, d))
+            for k, (weights, moving) in enumerate(pairs):
+                nc.tensor.matmul(bank[:], weights, moving, start=(k == 0), stop=(k == len(pairs) - 1))
+            nc.vector.scalar_tensor_tensor(
+                scaled[gate][:, d, :], bank[:], bias, q_sb[:, d * N : (d + 1) * N], ALU.add, ALU.mult
+            )
+
+        def mixed(gate):
             pre = held.tile([P, N], F32, name="pre_" + gate)
-            nc.vector.tensor_tensor(pre[:], scaled[:, 0, :], scaled[:, 1, :], ALU.add)
+            nc.vector.tensor_tensor(pre[:], scaled[gate][:, 0, :], scaled[gate][:, 1, :], ALU.add)
             return pre
 
-        def ru_gate(gate, g):
-            products = [
-                [(w_ru_sb[:, kb, (2 * d + g) * P : (2 * d + g + 1) * P], conv_sb[:, kb, :]) for kb in range(KB)]
-                for d in range(D)
-            ]
-            return mixed(gate, products, [biases[:, 2 * d + g : 2 * d + g + 1] for d in range(D)])
+        for d in range(D):
+            for g, gate in enumerate(("r", "u")):
+                product_and_scaling(
+                    gate,
+                    d,
+                    [(w_ru_sb[d][:, kb, g * P : (g + 1) * P], conv_sb[:, kb, :]) for kb in range(KB)],
+                    biases[:, 2 * d + g : 2 * d + g + 1],
+                )
 
-        pre_r = ru_gate("r", 0)
+        pre_r = mixed("r")
         r = held.tile([P, N], F32, name="r")
         nc.scalar.activation(r[:], pre_r[:], FUNC.Sigmoid)
 
-        pre_u = ru_gate("u", 1)
+        pre_u = mixed("u")
         one_minus_u = held.tile([P, N], F32, name="one_minus_u")
         nc.scalar.activation(one_minus_u[:], pre_u[:], FUNC.Sigmoid, scale=-1.0)
         u = held.tile([P, N], F32, name="u")
         nc.scalar.activation(u[:], pre_u[:], FUNC.Sigmoid)
 
-        pre_c = mixed(
-            "c",
-            [[(w_c_sb[:, d * P : (d + 1) * P], x_sb[:])] for d in range(D)],
-            [biases[:, 2 * D + d : 2 * D + d + 1] for d in range(D)],
-        )
+        for d in range(D):
+            product_and_scaling(
+                "c", d, [(w_c_sb[:, d * P : (d + 1) * P], x_sb[:])], biases[:, 2 * D + d : 2 * D + d + 1]
+            )
+        pre_c = mixed("c")
         cand = held.tile([P, N], F32, name="cand")
         nc.scalar.activation(cand[:], pre_c[:], FUNC.Tanh)
 

@@ -29,16 +29,16 @@ def tile_agcrncellwithmlp_kernel(tc, base, conv, x, h, q, w_ru, b_ru, w_c, b_c, 
         h_sb = held.tile([P, N], F32, name="h_sb")
         store = held.tile([P, S], F32, name="store")
 
-        w_ru_blocks = w_ru.rearrange("(kb p) e -> p kb e", p=P)
+        w_ru_blocks = w_ru.rearrange("(p kb) e -> p kb e", kb=KB)
         nc.sync.dma_start(q_row[:], q.rearrange("d j -> (d j)").unsqueeze(0))
         nc.scalar.dma_start(b_rows[0 : D * 2, :], b_ru.rearrange("(c p) o -> c (p o)", p=P))
         nc.sync.dma_start(w_ru_sb[0][:], w_ru_blocks[:, :, 0 : 2 * P])
         nc.scalar.dma_start(b_rows[D * 2 : D * 3, :], b_c.rearrange("(c p) o -> c (p o)", p=P))
         nc.sync.dma_start(w_ru_sb[1][:], w_ru_blocks[:, :, 2 * P : 4 * P])
-        nc.scalar.dma_start(conv_sb[:], conv.rearrange("(kb p) j -> p kb j", p=P))
-        nc.scalar.dma_start(h_sb[:], h)
+        nc.scalar.dma_start(conv_sb[:], conv.rearrange("(p kb) j -> p kb j", kb=KB))
         nc.sync.dma_start(w_c_sb[:], w_c)
         nc.sync.dma_start(x_sb[:], x)
+        nc.sync.dma_start(h_sb[:], h)
         nc.sync.dma_start(store[:], base)
         nc.sync.dma_start(offsets[:], offs)
 

import concourse.mybir as mybir

F32 = mybir.dt.float32
BF16 = mybir.dt.bfloat16
U16 = mybir.dt.uint16
ALU = mybir.AluOpType
FUNC = mybir.ActivationFunctionType

P = 128
N = 128
S = 256
D = 2
KB = 2
WARM_UP_PRODUCTS = 4

FLOPS = 2 * (KB * P) * (D * 2 * P) * N + 2 * P * (D * P) * N


def tile_agcrncellwithmlp_kernel(tc, base, conv, x, h, q, w_ru, b_ru, w_c, b_c, offs, out):
    nc = tc.nc
    with tc.tile_pool(name="held", bufs=1) as held, tc.psum_pool(name="psum", bufs=1) as psum:
        offsets = held.tile([P, N // 16], U16, name="offsets")
        w_ru_sb = [held.tile([P, KB, 2 * P], BF16, name="w_ru_sb%d" % d) for d in range(D)]
        conv_sb = held.tile([P, KB, N], BF16, name="conv_sb")
        q_row = held.tile([1, D * N], F32, name="q_row")
        b_rows = held.tile([D * 3, P], F32, name="b_rows")
        w_c_sb = held.tile([P, D * P], BF16, name="w_c_sb")
        x_sb = held.tile([P, N], BF16, name="x_sb")
        h_sb = held.tile([P, N], F32, name="h_sb")
        store = held.tile([P, S], F32, name="store")

        w_ru_blocks = w_ru.rearrange("(p kb) e -> p kb e", kb=KB)
        nc.sync.dma_start(q_row[:], q.rearrange("d j -> (d j)").unsqueeze(0))
        nc.scalar.dma_start(b_rows[0 : D * 2, :], b_ru.rearrange("(c p) o -> c (p o)", p=P))
        nc.sync.dma_start(w_ru_sb[0][:], w_ru_blocks[:, :, 0 : 2 * P])
        nc.scalar.dma_start(b_rows[D * 2 : D * 3, :], b_c.rearrange("(c p) o -> c (p o)", p=P))
        nc.sync.dma_start(w_ru_sb[1][:], w_ru_blocks[:, :, 2 * P : 4 * P])
        nc.scalar.dma_start(conv_sb[:], conv.rearrange("(p kb) j -> p kb j", kb=KB))
        nc.sync.dma_start(w_c_sb[:], w_c)
        nc.sync.dma_start(x_sb[:], x)
        nc.sync.dma_start(h_sb[:], h)
        nc.sync.dma_start(store[:], base)
        nc.sync.dma_start(offsets[:], offs)

        zeros = held.tile([P, D * N], BF16, name="zeros")
        nc.vector.memset(zeros[:], 0.0)
        q_bank = psum.tile([P, D * N], F32, name="q_bank")
        for i in range(WARM_UP_PRODUCTS):
            nc.tensor.matmul(q_bank[:], zeros[:, 0:P], zeros[:], start=True, stop=True)

        ones_row = held.tile([1, P], F32, name="ones_row")
        nc.vector.memset(ones_row[:], 1.0)
        identity = held.tile([D * 3, D * 3], F32, name="identity")
        nc.vector.memset(identity[:], 0.0)
        for k in range(D * 3):
            nc.vector.memset(identity[0 : k + 1, k : k + 1], 1.0)
        for k in range(1, D * 3):
            nc.vector.memset(identity[0:k, k : k + 1], 0.0)

        nc.tensor.matmul(q_bank[:], ones_row[:], q_row[:], start=True, stop=True)
        q_sb = held.tile([P, D * N], F32, name="q_sb")
        nc.vector.tensor_copy(q_sb[:], q_bank[:])

        bias_bank = psum.tile([P, D * 3], F32, name="bias_bank")
        nc.tensor.matmul(bias_bank[:], b_rows[:], identity[:], start=True, stop=True)
        biases = held.tile([P, D * 3], F32, name="biases")
        nc.vector.tensor_copy(biases[:], bias_bank[:])

        scaled = {}
        for gate in ("r", "u", "c"):
            scaled[gate] = held.tile([P, D, N], F32, name="scaled_" + gate)

        def product_and_scaling(gate, d, pairs, bias):
            bank = psum.tile([P, N], F32, name="bank_%s%d" % (gate, d))
            for k, (weights, moving) in enumerate(pairs):
                nc.tensor.matmul(bank[:], weights, moving, start=(k == 0), stop=(k == len(pairs) - 1))
            nc.vector.scalar_tensor_tensor(
                scaled[gate][:, d, :], bank[:], bias, q_sb[:, d * N : (d + 1) * N], ALU.add, ALU.mult
            )

        def mixed(gate):
            pre = held.tile([P, N], F32, name="pre_" + gate)
            nc.vector.tensor_tensor(pre[:], scaled[gate][:, 0, :], scaled[gate][:, 1, :], ALU.add)
            return pre

        for d in range(D):
            for g, gate in enumerate(("r", "u")):
                product_and_scaling(
                    gate,
                    d,
                    [(w_ru_sb[d][:, kb, g * P : (g + 1) * P], conv_sb[:, kb, :]) for kb in range(KB)],
                    biases[:, 2 * d + g : 2 * d + g + 1],
                )

        pre_r = mixed("r")
        r = held.tile([P, N], F32, name="r")
        nc.scalar.activation(r[:], pre_r[:], FUNC.Sigmoid)

        pre_u = mixed("u")
        one_minus_u = held.tile([P, N], F32, name="one_minus_u")
        nc.scalar.activation(one_minus_u[:], pre_u[:], FUNC.Sigmoid, scale=-1.0)
        u = held.tile([P, N], F32, name="u")
        nc.scalar.activation(u[:], pre_u[:], FUNC.Sigmoid)

        for d in range(D):
            product_and_scaling(
                "c", d, [(w_c_sb[:, d * P : (d + 1) * P], x_sb[:])], biases[:, 2 * D + d : 2 * D + d + 1]
            )
        pre_c = mixed("c")
        cand = held.tile([P, N], F32, name="cand")
        nc.scalar.activation(cand[:], pre_c[:], FUNC.Tanh)

        r_h = held.tile([P, N], F32, name="r_h")
        nc.vector.tensor_tensor(r_h[:], r[:], h_sb[:], ALU.mult)
        kept = held.tile([P, N], F32, name="kept")
        nc.vector.tensor_tensor(kept[:], one_minus_u[:], r_h[:], ALU.mult)
        fresh = held.tile([P, N], F32, name="fresh")
        nc.vector.tensor_tensor(fresh[:], u[:], cand[:], ALU.mult)
        nc.vector.tensor_tensor(store[:].indirect(offsets[:]), kept[:], fresh[:], ALU.add)

        nc.sync.dma_start(out, store[:])
